import numpy as np
import ml_dtypes


def mxq(x, axis, fmt="e4m3"):
    dtype, down = {"e4m3": (ml_dtypes.float8_e4m3fn, 7), "e5m2": (ml_dtypes.float8_e5m2, 14)}[fmt]
    v = np.moveaxis(np.asarray(x, np.float32).astype(ml_dtypes.bfloat16).astype(np.float64), axis, -1)
    blocks = v.reshape(v.shape[:-1] + (-1, 32))
    amax = np.abs(blocks).max(-1, keepdims=True)
    byte = np.maximum(np.where(amax > 0, np.frexp(amax)[1] - 1 + 127, 0) - down, 1)
    scale = np.exp2(byte - 127.0)
    codes = (blocks / scale).astype(np.float32).astype(dtype).astype(np.float64)
    return np.moveaxis((codes * scale).reshape(v.shape), -1, axis)


WIDE = False


def mx_kscale(k):
    if not WIDE:
        return np.ones(k)
    levels = np.array([10, -10, 5, -5, 0])
    a = np.random.permutation(np.resize(levels, k // 512 * 4)).reshape(k // 512, 4)
    idx = np.arange(k)
    return np.exp2(a[idx // 512, idx % 128 // 32])


BF16 = ml_dtypes.bfloat16


def bf(x):
    return np.asarray(x, np.float32).astype(BF16)


def f64(x):
    return np.asarray(x).astype(np.float64)


E2M1 = np.array([0.0, 0.5, 1.0, 1.5, 2.0, 3.0, 4.0, 6.0, -0.0, -0.5, -1.0, -1.5, -2.0, -3.0, -4.0, -6.0])


def pack_weight(w, fmt):
    k, n = w.shape
    w = f64(bf(w)).reshape(k // 32, 32, n)
    amax = np.abs(w).max(1)
    if fmt == "e4m3":
        byte = np.frexp(amax)[1] - 1 + 127 - 7
    else:
        mant, ex = np.frexp(amax / 6.0)
        byte = np.where(mant > 0.5, ex, ex - 1) + 127
    byte = np.clip(np.where(amax > 0, byte, 1), 1, 254)
    scaled = (w * np.exp2(127.0 - byte)[:, None, :]).reshape(k, n).astype(np.float32)
    by_word = np.ascontiguousarray(scaled.reshape(k // 512, 128, 4, n).transpose(0, 1, 3, 2))
    if fmt == "e4m3":
        words = by_word.astype(ml_dtypes.float8_e4m3fn).view(np.uint8)
    else:
        c = by_word.astype(ml_dtypes.float4_e2m1fn).view(np.uint8) & 0xF
        words = c[..., 0::2] | (c[..., 1::2] << 4)
    return np.ascontiguousarray(words), np.ascontiguousarray(byte.astype(np.uint8).reshape(k // 512, 16, n))


def unpack_weight(words, scales, fmt):
    g, p, n, _ = words.shape
    if fmt == "e4m3":
        vals = np.ascontiguousarray(words).view(ml_dtypes.float8_e4m3fn).astype(np.float64)
    else:
        nib = np.empty((g, p, n, 4), np.uint8)
        nib[..., 0::2] = words & 0xF
        nib[..., 1::2] = words >> 4
        vals = E2M1[nib]
    vals = vals * np.repeat(np.exp2(scales.astype(np.float64) - 127.0), 8, axis=1)[..., None]
    return vals.transpose(0, 1, 3, 2).reshape(g * 512, n)

def pack4(w):
    words, scales = pack_weight(w, "e2m1")
    return words.reshape(words.shape[0], 128, -1), scales


def unpack4(words, scales):
    return unpack_weight(words.reshape(words.shape[0], 128, -1, 2), scales, "e2m1")


B, T, G, I, H = 2, 64, 2, 4096, 3072


def setup_inputs():
    s = mx_kscale(I)
    x = bf((np.random.standard_normal((B, T, G, I)) * s).reshape(B, T, G * I))
    w = np.random.standard_normal((G, H, I)) / np.sqrt(I) / s
    stack = np.swapaxes(w, 1, 2)
    words, scales = pack4(stack.reshape(-1, H))
    b = bf(np.random.standard_normal((G, H)) * 0.5)
    return {"x": x, "W_words": words, "W_scales": scales, "b": b}


def reference(x, W_words, W_scales, b):
    xg = f64(x).reshape(B, T, G, I)
    xq = mxq(xg, 3, "e4m3")
    wq = unpack4(W_words, W_scales).reshape(G, I, H)
    y = xq.transpose(2, 0, 1, 3).reshape(G, B * T, I) @ wq
    out = y.reshape(G, B, T, H).transpose(1, 2, 0, 3) + f64(b)
    return np.swapaxes(out, -1, -2).reshape(B, T, G * H)

@@ -1,0 +1,174 @@
+from contextlib import ExitStack
+
+import concourse.mybir as mybir
+from concourse.masks import make_identity
+
+F32 = mybir.dt.float32
+BF16 = mybir.dt.bfloat16
+I32 = mybir.dt.int32
+U8 = mybir.dt.uint8
+U32 = mybir.dt.uint32
+FP8X4 = mybir.dt.float8_e4m3fn_x4
+FP4X4 = mybir.dt.float4_e2m1fn_x4
+
+P = 128
+GROUPS = 2
+IN = 4096
+OUT = 3072
+K_PASS = 512
+PASSES = IN // K_PASS
+BANK = 512
+CHUNKS = OUT // BANK
+X_PIECES = 4
+PIECE_PASSES = GROUPS * PASSES // X_PIECES
+PAIRS = GROUPS * PASSES // 2
+WORD_BUFS = 8
+
+FLOPS = 2 * P * GROUPS * IN * OUT
+
+
+def tile_groupedlinear_w_e_kernel(tc, x, W_words, W_scales, b, out):
+    nc = tc.nc
+    x_rows = x.flatten_outer_dims()
+    out_rows = out.flatten_outer_dims()
+    scale_rows = W_scales.bitcast(I32).rearrange("g q n -> q g n")
+
+    with ExitStack() as ctx:
+        ctx.enter_context(tc.manual_schedule())
+        keep = ctx.enter_context(tc.tile_pool(name="keep", bufs=1))
+        x_pool = ctx.enter_context(tc.tile_pool(name="x_pool", bufs=X_PIECES))
+        grouped_pool = ctx.enter_context(tc.tile_pool(name="grouped_pool", bufs=3))
+        word_pool = ctx.enter_context(tc.tile_pool(name="word_pool", bufs=WORD_BUFS))
+        out_pool = ctx.enter_context(tc.tile_pool(name="out_pool", bufs=3))
+        psum = ctx.enter_context(tc.psum_pool(name="psum", bufs=8))
+
+        ident_f32 = keep.tile([P, P], F32, name="ident_f32")
+        ident_bf16 = keep.tile([P, P], BF16, name="ident_bf16")
+        bias_rows = keep.tile([P, BANK], BF16, name="bias_rows")
+        bias_all = keep.tile([P, GROUPS, OUT], F32, name="bias_all")
+        x_codes = keep.tile([P, GROUPS * PASSES * P], U32, name="x_codes", align_bytes=64)
+        x_planes = keep.tile([P, GROUPS * PASSES * P], U8, name="x_planes", align_bytes=64)
+        w_planes = keep.tile([P, GROUPS * PASSES, OUT], U8, name="w_planes", align_bytes=64)
+        y_all = keep.tile([P, GROUPS, OUT], F32, name="y_all")
+
+        make_identity(nc, ident_f32[:])
+        make_identity(nc, ident_bf16[:])
+
+        def zero_scale_planes(e):
+            planes = w_planes[:, e * PASSES : (e + 1) * PASSES, :]
+            nc.vector.memset(planes.bitcast(I32), 0)
+
+        def load_scale_rows(first_pass, last_pass):
+            for half in range(2):
+                for r in range(4):
+                    nc.sync.dma_start(
+                        out=w_planes[32 * half + r : P : 64, first_pass:last_pass, :].bitcast(I32),
+                        in_=scale_rows[4 * half + r : 16 : 8, first_pass:last_pass, :],
+                    )
+
+        def load_group_scales(e):
+            first = e * PASSES
+            load_scale_rows(first, first + PASSES - 1)
+            load_scale_rows(first + PASSES - 1, first + PASSES)
+
+        def load_group_words(e):
+            tiles = []
+            for g in range(e * PASSES, (e + 1) * PASSES):
+                words = word_pool.tile([P, 2 * OUT], U8, name="words", tag="words", align_bytes=64)
+                nc.sync.dma_start(out=words[:].bitcast(I32), in_=W_words[g].bitcast(I32))
+                tiles.append(words)
+            return tiles
+
+        nc.vector.memset(bias_rows[:], 0.0)
+        zero_scale_planes(0)
+        nc.sync.dma_start(
+            out=bias_rows[0 : GROUPS * CHUNKS, :], in_=b.rearrange("e (c n) -> (e c) n", n=BANK)
+        )
+        x_tiles = []
+        piece_cols = PIECE_PASSES * K_PASS
+        for i in range(X_PIECES):
+            x_piece = x_pool.tile([P, piece_cols], BF16, name="x_piece", tag="x_piece")
+            nc.sync.dma_start(out=x_piece[:], in_=x_rows[:, i * piece_cols : (i + 1) * piece_cols])
+            x_tiles.append(x_piece)
+        load_group_scales(0)
+        word_tiles = load_group_words(0)
+
+        def quantise_pair(j, grouped):
+            cols = slice(j * 2 * P, (j + 1) * 2 * P)
+            nc.vector.quantize_mx(
+                out=x_codes[:, cols].bitcast(FP8X4), scales=x_planes[:, cols], in_=grouped[:]
+            )
+
+        waiting = None
+        for j in range(PAIRS):
+            x_words = x_tiles[2 * j // PIECE_PASSES][:].bitcast(F32)
+            xt = psum.tile([P, BANK], F32, name="xt", tag="bank")
+            for s in range(2):
+                local = (2 * j + s) % PIECE_PASSES
+                for u in range(2):
+                    nc.tensor.transpose(
+                        xt[:, (2 * s + u) * P : (2 * s + u + 1) * P],
+                        x_words[:, 256 * local + u : 256 * (local + 1) : 2],
+                        ident_f32[:],
+                    )
+            grouped = grouped_pool.tile([P, 2 * K_PASS], BF16, name="grouped", tag="grouped", align_bytes=64)
+            dst = grouped[:].bitcast(F32).rearrange("p (s r u) -> p s r u", s=2, u=2)
+            src = xt[:].rearrange("p (s u r) -> p s r u", s=2, u=2)
+            if j % 2 == 0:
+                nc.scalar.copy(out=dst, in_=src)
+            else:
+                nc.vector.tensor_copy(out=dst, in_=src)
+            if waiting is not None:
+                quantise_pair(j - 1, waiting)
+            waiting = grouped
+        quantise_pair(PAIRS - 1, waiting)
+
+        for k in range(GROUPS * CHUNKS):
+            spread = psum.tile([P, BANK], F32, name="spread", tag="bank")
+            nc.tensor.matmul(
+                out=spread[:],
+                lhsT=ident_bf16[:, k : k + 1].to_broadcast([P, P]),
+                rhs=bias_rows[:],
+                start=True,
+                stop=True,
+            )
+            dst = bias_all[:, k // CHUNKS, (k % CHUNKS) * BANK : (k % CHUNKS + 1) * BANK]
+            if k % 2 == 0:
+                nc.scalar.copy(out=dst, in_=spread[:])
+            else:
+                nc.vector.tensor_copy(out=dst, in_=spread[:])
+        zero_scale_planes(1)
+
+        for e in range(GROUPS):
+            if e + 1 < GROUPS:
+                load_group_scales(e + 1)
+                next_word_tiles = load_group_words(e + 1)
+            acc = [psum.tile([P, BANK], F32, name="acc", tag="bank") for c in range(CHUNKS)]
+            for s in range(PASSES):
+                g = e * PASSES + s
+                for c in range(CHUNKS):
+                    nc.tensor.matmul_mx(
+                        out=acc[c][:],
+                        lhsT=x_codes[:, g * P : (g + 1) * P].bitcast(FP8X4),
+                        lhsT_scale=x_planes[:, g * P : (g + 1) * P],
+                        rhs=word_tiles[s][:, c * 2 * BANK : (c + 1) * 2 * BANK].bitcast(FP4X4),
+                        rhs_scale=w_planes[:, g, c * BANK : (c + 1) * BANK],
+                        start=(s == 0),
+                        stop=(s == PASSES - 1),
+                    )
+            for c in range(CHUNKS):
+                cols = slice(c * BANK, (c + 1) * BANK)
+                nc.vector.tensor_tensor(
+                    out=y_all[:, e, cols], in0=acc[c][:], in1=bias_all[:, e, cols], op=mybir.AluOpType.add
+                )
+                if e == GROUPS - 1:
+                    shuffled = out_pool.tile([P, GROUPS * BANK], F32, name="shuffled", tag="shuffled")
+                    nc.scalar.copy(
+                        out=shuffled[:].rearrange("p (h e) -> p h e", e=GROUPS),
+                        in_=y_all[:, :, cols].rearrange("p e h -> p h e"),
+                    )
+                    nc.sync.dma_start(
+                        out=out_rows[:, c * GROUPS * BANK : (c + 1) * GROUPS * BANK], in_=shuffled[:]
+                    )
+            if e + 1 < GROUPS:
+                word_tiles = next_word_tiles

@@ -23,6 +23,8 @@ X_PIECES = 4
 PIECE_PASSES = GROUPS * PASSES // X_PIECES
 PAIRS = GROUPS * PASSES // 2
 WORD_BUFS = 8
+LAST_PARTS = 2
+PART_BUFS = 12
 
 FLOPS = 2 * P * GROUPS * IN * OUT
 
@@ -39,44 +41,56 @@ def tile_groupedlinear_w_e_kernel(tc, x, W_words, W_scales, b, out):
         x_pool = ctx.enter_context(tc.tile_pool(name="x_pool", bufs=X_PIECES))
         grouped_pool = ctx.enter_context(tc.tile_pool(name="grouped_pool", bufs=3))
         word_pool = ctx.enter_context(tc.tile_pool(name="word_pool", bufs=WORD_BUFS))
-        out_pool = ctx.enter_context(tc.tile_pool(name="out_pool", bufs=3))
+        part_pool = ctx.enter_context(tc.tile_pool(name="part_pool", bufs=PART_BUFS))
+        out_pool = ctx.enter_context(tc.tile_pool(name="out_pool", bufs=CHUNKS))
         psum = ctx.enter_context(tc.psum_pool(name="psum", bufs=8))
 
         ident_f32 = keep.tile([P, P], F32, name="ident_f32")
         ident_bf16 = keep.tile([P, P], BF16, name="ident_bf16")
         bias_rows = keep.tile([P, BANK], BF16, name="bias_rows")
-        bias_all = keep.tile([P, GROUPS, OUT], F32, name="bias_all")
+        bias_all = keep.tile([P, GROUPS, OUT], BF16, name="bias_all")
         x_codes = keep.tile([P, GROUPS * PASSES * P], U32, name="x_codes", align_bytes=64)
         x_planes = keep.tile([P, GROUPS * PASSES * P], U8, name="x_planes", align_bytes=64)
-        w_planes = keep.tile([P, GROUPS * PASSES, OUT], U8, name="w_planes", align_bytes=64)
+        w_planes = [
+            keep.tile([P, PASSES, OUT], U8, name="w_planes%d" % e, align_bytes=64) for e in range(GROUPS)
+        ]
         y_all = keep.tile([P, GROUPS, OUT], F32, name="y_all")
 
         make_identity(nc, ident_f32[:])
         make_identity(nc, ident_bf16[:])
 
         def zero_scale_planes(e):
-            planes = w_planes[:, e * PASSES : (e + 1) * PASSES, :]
-            nc.vector.memset(planes.bitcast(I32), 0)
+            nc.vector.memset(w_planes[e][:].bitcast(I32), 0)
 
-        def load_scale_rows(first_pass, last_pass):
+        def load_scale_rows(e, first, last):
             for half in range(2):
                 for r in range(4):
                     nc.sync.dma_start(
-                        out=w_planes[32 * half + r : P : 64, first_pass:last_pass, :].bitcast(I32),
-                        in_=scale_rows[4 * half + r : 16 : 8, first_pass:last_pass, :],
+                        out=w_planes[e][32 * half + r : P : 64, first:last, :].bitcast(I32),
+                        in_=scale_rows[4 * half + r : 16 : 8, e * PASSES + first : e * PASSES + last, :],
                     )
 
         def load_group_scales(e):
-            first = e * PASSES
-            load_scale_rows(first, first + PASSES - 1)
-            load_scale_rows(first + PASSES - 1, first + PASSES)
+            load_scale_rows(e, 0, PASSES - 1)
+            load_scale_rows(e, PASSES - 1, PASSES)
+
+        def column_parts(e):
+            return LAST_PARTS if e == GROUPS - 1 else 1
 
         def load_group_words(e):
+            parts = column_parts(e)
+            pool = word_pool if parts == 1 else part_pool
+            width = 2 * OUT // parts
             tiles = []
-            for g in range(e * PASSES, (e + 1) * PASSES):
-                words = word_pool.tile([P, 2 * OUT], U8, name="words", tag="words", align_bytes=64)
-                nc.sync.dma_start(out=words[:].bitcast(I32), in_=W_words[g].bitcast(I32))
-                tiles.append(words)
+            for part in range(parts):
+                tiles.append([])
+                for g in range(e * PASSES, (e + 1) * PASSES):
+                    words = pool.tile([P, width], U8, name="words", tag="words", align_bytes=64)
+                    nc.sync.dma_start(
+                        out=words[:].bitcast(I32),
+                        in_=W_words[g, :, part * width : (part + 1) * width].bitcast(I32),
+                    )
+                    tiles[part].append(words)
             return tiles
 
         nc.vector.memset(bias_rows[:], 0.0)
@@ -143,32 +157,37 @@ def tile_groupedlinear_w_e_kernel(tc, x, W_words, W_scales, b, out):
             if e + 1 < GROUPS:
                 load_group_scales(e + 1)
                 next_word_tiles = load_group_words(e + 1)
-            acc = [psum.tile([P, BANK], F32, name="acc", tag="bank") for c in range(CHUNKS)]
-            for s in range(PASSES):
-                g = e * PASSES + s
-                for c in range(CHUNKS):
-                    nc.tensor.matmul_mx(
-                        out=acc[c][:],
-                        lhsT=x_codes[:, g * P : (g + 1) * P].bitcast(FP8X4),
-                        lhsT_scale=x_planes[:, g * P : (g + 1) * P],
-                        rhs=word_tiles[s][:, c * 2 * BANK : (c + 1) * 2 * BANK].bitcast(FP4X4),
-                        rhs_scale=w_planes[:, g, c * BANK : (c + 1) * BANK],
-                        start=(s == 0),
-                        stop=(s == PASSES - 1),
+            parts = column_parts(e)
+            for part in range(parts):
+                chunks = range(part * CHUNKS // parts, (part + 1) * CHUNKS // parts)
+                acc = [psum.tile([P, BANK], F32, name="acc", tag="bank") for c in chunks]
+                for s in range(PASSES):
+                    g = e * PASSES + s
+                    for i, c in enumerate(chunks):
+                        nc.tensor.matmul_mx(
+                            out=acc[i][:],
+                            lhsT=x_codes[:, g * P : (g + 1) * P].bitcast(FP8X4),
+                            lhsT_scale=x_planes[:, g * P : (g + 1) * P],
+                            rhs=word_tiles[part][s][:, i * 2 * BANK : (i + 1) * 2 * BANK].bitcast(FP4X4),
+                            rhs_scale=w_planes[e][:, s, c * BANK : (c + 1) * BANK],
+                            start=(s == 0),
+                            stop=(s == PASSES - 1),
+                        )
+                for i, c in enumerate(chunks):
+                    cols = slice(c * BANK, (c + 1) * BANK)
+                    nc.vector.tensor_tensor(
+                        out=y_all[:, e, cols], in0=acc[i][:], in1=bias_all[:, e, cols], op=mybir.AluOpType.add
                     )
-            for c in range(CHUNKS):
-                cols = slice(c * BANK, (c + 1) * BANK)
-                nc.vector.tensor_tensor(
-                    out=y_all[:, e, cols], in0=acc[c][:], in1=bias_all[:, e, cols], op=mybir.AluOpType.add
-                )
-                if e == GROUPS - 1:
-                    shuffled = out_pool.tile([P, GROUPS * BANK], F32, name="shuffled", tag="shuffled")
-                    nc.scalar.copy(
-                        out=shuffled[:].rearrange("p (h e) -> p h e", e=GROUPS),
-                        in_=y_all[:, :, cols].rearrange("p e h -> p h e"),
-                    )
-                    nc.sync.dma_start(
-                        out=out_rows[:, c * GROUPS * BANK : (c + 1) * GROUPS * BANK], in_=shuffled[:]
-                    )
+                    if e == GROUPS - 1:
+                        shuffled = out_pool.tile([P, GROUPS * BANK], F32, name="shuffled", tag="shuffled")
+                        dst = shuffled[:].rearrange("p (h e) -> p h e", e=GROUPS)
+                        src = y_all[:, :, cols].rearrange("p e h -> p h e")
+                        if c % 2 == 0:
+                            nc.scalar.copy(out=dst, in_=src)
+                        else:
+                            nc.vector.tensor_copy(out=dst, in_=src)
+                        nc.sync.dma_start(
+                            out=out_rows[:, c * GROUPS * BANK : (c + 1) * GROUPS * BANK], in_=shuffled[:]
+                        )
             if e + 1 < GROUPS:
                 word_tiles = next_word_tiles

@@ -19,8 +19,6 @@ K_PASS = 512
 PASSES = IN // K_PASS
 BANK = 512
 CHUNKS = OUT // BANK
-X_PIECES = 4
-PIECE_PASSES = GROUPS * PASSES // X_PIECES
 PAIRS = GROUPS * PASSES // 2
 WORD_BUFS = 8
 LAST_PARTS = 2
@@ -38,13 +36,13 @@ def tile_groupedlinear_w_e_kernel(tc, x, W_words, W_scales, b, out):
     with ExitStack() as ctx:
         ctx.enter_context(tc.manual_schedule())
         keep = ctx.enter_context(tc.tile_pool(name="keep", bufs=1))
-        x_pool = ctx.enter_context(tc.tile_pool(name="x_pool", bufs=X_PIECES))
         grouped_pool = ctx.enter_context(tc.tile_pool(name="grouped_pool", bufs=3))
         word_pool = ctx.enter_context(tc.tile_pool(name="word_pool", bufs=WORD_BUFS))
         part_pool = ctx.enter_context(tc.tile_pool(name="part_pool", bufs=PART_BUFS))
         out_pool = ctx.enter_context(tc.tile_pool(name="out_pool", bufs=CHUNKS))
         psum = ctx.enter_context(tc.psum_pool(name="psum", bufs=8))
 
+        x_all = keep.tile([P, GROUPS * IN], BF16, name="x_all")
         ident_f32 = keep.tile([P, P], F32, name="ident_f32")
         ident_bf16 = keep.tile([P, P], BF16, name="ident_bf16")
         bias_rows = keep.tile([P, BANK], BF16, name="bias_rows")
@@ -70,10 +68,6 @@ def tile_groupedlinear_w_e_kernel(tc, x, W_words, W_scales, b, out):
                         in_=scale_rows[4 * half + r : 16 : 8, e * PASSES + first : e * PASSES + last, :],
                     )
 
-        def load_group_scales(e):
-            load_scale_rows(e, 0, PASSES - 1)
-            load_scale_rows(e, PASSES - 1, PASSES)
-
         def column_parts(e):
             return LAST_PARTS if e == GROUPS - 1 else 1
 
@@ -93,19 +87,18 @@ def tile_groupedlinear_w_e_kernel(tc, x, W_words, W_scales, b, out):
                     tiles[part].append(words)
             return tiles
 
+        nc.sync.dma_start(out=x_all[:], in_=x_rows)
         nc.vector.memset(bias_rows[:], 0.0)
-        zero_scale_planes(0)
         nc.sync.dma_start(
             out=bias_rows[0 : GROUPS * CHUNKS, :], in_=b.rearrange("e (c n) -> (e c) n", n=BANK)
         )
-        x_tiles = []
-        piece_cols = PIECE_PASSES * K_PASS
-        for i in range(X_PIECES):
-            x_piece = x_pool.tile([P, piece_cols], BF16, name="x_piece", tag="x_piece")
-            nc.sync.dma_start(out=x_piece[:], in_=x_rows[:, i * piece_cols : (i + 1) * piece_cols])
-            x_tiles.append(x_piece)
-        load_group_scales(0)
-        word_tiles = load_group_words(0)
+        for e in range(GROUPS):
+            zero_scale_planes(e)
+        for e in range(GROUPS - 1):
+            load_scale_rows(e, 0, PASSES)
+        load_scale_rows(GROUPS - 1, 0, PASSES - 1)
+        load_scale_rows(GROUPS - 1, PASSES - 1, PASSES)
+        word_tiles = [load_group_words(e) for e in range(GROUPS)]
 
         def quantise_pair(j, grouped):
             cols = slice(j * 2 * P, (j + 1) * 2 * P)
@@ -113,16 +106,16 @@ def tile_groupedlinear_w_e_kernel(tc, x, W_words, W_scales, b, out):
                 out=x_codes[:, cols].bitcast(FP8X4), scales=x_planes[:, cols], in_=grouped[:]
             )
 
+        x_words = x_all[:].bitcast(F32)
         waiting = None
         for j in range(PAIRS):
-            x_words = x_tiles[2 * j // PIECE_PASSES][:].bitcast(F32)
             xt = psum.tile([P, BANK], F32, name="xt", tag="bank")
             for s in range(2):
-                local = (2 * j + s) % PIECE_PASSES
+                g = 2 * j + s
                 for u in range(2):
                     nc.tensor.transpose(
                         xt[:, (2 * s + u) * P : (2 * s + u + 1) * P],
-                        x_words[:, 256 * local + u : 256 * (local + 1) : 2],
+                        x_words[:, 256 * g + u : 256 * (g + 1) : 2],
                         ident_f32[:],
                     )
             grouped = grouped_pool.tile([P, 2 * K_PASS], BF16, name="grouped", tag="grouped", align_bytes=64)
@@ -151,12 +144,8 @@ def tile_groupedlinear_w_e_kernel(tc, x, W_words, W_scales, b, out):
                 nc.scalar.copy(out=dst, in_=spread[:])
             else:
                 nc.vector.tensor_copy(out=dst, in_=spread[:])
-        zero_scale_planes(1)
 
         for e in range(GROUPS):
-            if e + 1 < GROUPS:
-                load_group_scales(e + 1)
-                next_word_tiles = load_group_words(e + 1)
             parts = column_parts(e)
             for part in range(parts):
                 chunks = range(part * CHUNKS // parts, (part + 1) * CHUNKS // parts)
@@ -168,7 +157,7 @@ def tile_groupedlinear_w_e_kernel(tc, x, W_words, W_scales, b, out):
                             out=acc[i][:],
                             lhsT=x_codes[:, g * P : (g + 1) * P].bitcast(FP8X4),
                             lhsT_scale=x_planes[:, g * P : (g + 1) * P],
-                            rhs=word_tiles[part][s][:, i * 2 * BANK : (i + 1) * 2 * BANK].bitcast(FP4X4),
+                            rhs=word_tiles[e][part][s][:, i * 2 * BANK : (i + 1) * 2 * BANK].bitcast(FP4X4),
                             rhs_scale=w_planes[e][:, s, c * BANK : (c + 1) * BANK],
                             start=(s == 0),
                             stop=(s == PASSES - 1),
@@ -189,5 +178,3 @@ def tile_groupedlinear_w_e_kernel(tc, x, W_words, W_scales, b, out):
                         nc.sync.dma_start(
                             out=out_rows[:, c * GROUPS * BANK : (c + 1) * GROUPS * BANK], in_=shuffled[:]
                         )
-            if e + 1 < GROUPS:
-                word_tiles = next_word_tiles

@@ -23,6 +23,7 @@ PAIRS = GROUPS * PASSES // 2
 WORD_BUFS = 8
 LAST_PARTS = 2
 PART_BUFS = 12
+LAST_RUN_PASSES = 3
 
 FLOPS = 2 * P * GROUPS * IN * OUT
 
@@ -96,8 +97,8 @@ def tile_groupedlinear_w_e_kernel(tc, x, W_words, W_scales, b, out):
             zero_scale_planes(e)
         for e in range(GROUPS - 1):
             load_scale_rows(e, 0, PASSES)
-        load_scale_rows(GROUPS - 1, 0, PASSES - 1)
-        load_scale_rows(GROUPS - 1, PASSES - 1, PASSES)
+        load_scale_rows(GROUPS - 1, 0, PASSES - LAST_RUN_PASSES)
+        load_scale_rows(GROUPS - 1, PASSES - LAST_RUN_PASSES, PASSES)
         word_tiles = [load_group_words(e) for e in range(GROUPS)]
 
         def quantise_pair(j, grouped):

@@ -90,14 +90,14 @@ def tile_groupedlinear_w_e_kernel(tc, x, W_words, W_scales, b, out):
 
         nc.sync.dma_start(out=x_all[:], in_=x_rows)
         nc.vector.memset(bias_rows[:], 0.0)
-        nc.sync.dma_start(
-            out=bias_rows[0 : GROUPS * CHUNKS, :], in_=b.rearrange("e (c n) -> (e c) n", n=BANK)
-        )
         for e in range(GROUPS):
             zero_scale_planes(e)
         for e in range(GROUPS - 1):
             load_scale_rows(e, 0, PASSES)
         load_scale_rows(GROUPS - 1, 0, PASSES - LAST_RUN_PASSES)
+        nc.sync.dma_start(
+            out=bias_rows[0 : GROUPS * CHUNKS, :], in_=b.rearrange("e (c n) -> (e c) n", n=BANK)
+        )
         load_scale_rows(GROUPS - 1, PASSES - LAST_RUN_PASSES, PASSES)
         word_tiles = [load_group_words(e) for e in range(GROUPS)]
 

@@ -20,9 +20,8 @@ PASSES = IN // K_PASS
 BANK = 512
 CHUNKS = OUT // BANK
 PAIRS = GROUPS * PASSES // 2
-WORD_BUFS = 8
-LAST_PARTS = 2
-PART_BUFS = 12
+WORD_BUFS = 7
+LAST_SPLIT = (4, 2)
 LAST_RUN_PASSES = 3
 
 FLOPS = 2 * P * GROUPS * IN * OUT
@@ -39,7 +38,7 @@ def tile_groupedlinear_w_e_kernel(tc, x, W_words, W_scales, b, out):
         keep = ctx.enter_context(tc.tile_pool(name="keep", bufs=1))
         grouped_pool = ctx.enter_context(tc.tile_pool(name="grouped_pool", bufs=3))
         word_pool = ctx.enter_context(tc.tile_pool(name="word_pool", bufs=WORD_BUFS))
-        part_pool = ctx.enter_context(tc.tile_pool(name="part_pool", bufs=PART_BUFS))
+        part_pool = ctx.enter_context(tc.tile_pool(name="part_pool", bufs=PASSES))
         out_pool = ctx.enter_context(tc.tile_pool(name="out_pool", bufs=CHUNKS))
         psum = ctx.enter_context(tc.psum_pool(name="psum", bufs=8))
 
@@ -70,22 +69,27 @@ def tile_groupedlinear_w_e_kernel(tc, x, W_words, W_scales, b, out):
                     )
 
         def column_parts(e):
-            return LAST_PARTS if e == GROUPS - 1 else 1
+            if e < GROUPS - 1:
+                return [range(CHUNKS)]
+            firsts = [sum(LAST_SPLIT[:i]) for i in range(len(LAST_SPLIT))]
+            return [range(first, first + count) for first, count in zip(firsts, LAST_SPLIT)]
 
         def load_group_words(e):
-            parts = column_parts(e)
-            pool = word_pool if parts == 1 else part_pool
-            width = 2 * OUT // parts
             tiles = []
-            for part in range(parts):
+            for part, chunks in enumerate(column_parts(e)):
+                first_byte = chunks.start * 2 * BANK
+                width = len(chunks) * 2 * BANK
                 tiles.append([])
                 for g in range(e * PASSES, (e + 1) * PASSES):
-                    words = pool.tile([P, width], U8, name="words", tag="words", align_bytes=64)
+                    if len(chunks) == CHUNKS:
+                        words = word_pool.tile([P, width], U8, name="words", tag="words", align_bytes=64)
+                    else:
+                        words = part_pool.tile([P, width], U8, name="words", tag="words%d" % part, align_bytes=64)
                     nc.sync.dma_start(
                         out=words[:].bitcast(I32),
-                        in_=W_words[g, :, part * width : (part + 1) * width].bitcast(I32),
+                        in_=W_words[g, :, first_byte : first_byte + width].bitcast(I32),
                     )
-                    tiles[part].append(words)
+                    tiles[-1].append(words)
             return tiles
 
         nc.sync.dma_start(out=x_all[:], in_=x_rows)
@@ -147,9 +151,7 @@ def tile_groupedlinear_w_e_kernel(tc, x, W_words, W_scales, b, out):
                 nc.vector.tensor_copy(out=dst, in_=spread[:])
 
         for e in range(GROUPS):
-            parts = column_parts(e)
-            for part in range(parts):
-                chunks = range(part * CHUNKS // parts, (part + 1) * CHUNKS // parts)
+            for part, chunks in enumerate(column_parts(e)):
                 acc = [psum.tile([P, BANK], F32, name="acc", tag="bank") for c in chunks]
                 for s in range(PASSES):
                     g = e * PASSES + s

@@ -22,6 +22,7 @@ CHUNKS = OUT // BANK
 PAIRS = GROUPS * PASSES // 2
 WORD_BUFS = 7
 LAST_SPLIT = (4, 2)
+ALIGN = 256
 LAST_RUN_PASSES = 3
 
 FLOPS = 2 * P * GROUPS * IN * OUT
@@ -42,17 +43,17 @@ def tile_groupedlinear_w_e_kernel(tc, x, W_words, W_scales, b, out):
         out_pool = ctx.enter_context(tc.tile_pool(name="out_pool", bufs=CHUNKS))
         psum = ctx.enter_context(tc.psum_pool(name="psum", bufs=8))
 
-        x_all = keep.tile([P, GROUPS * IN], BF16, name="x_all")
-        ident_f32 = keep.tile([P, P], F32, name="ident_f32")
-        ident_bf16 = keep.tile([P, P], BF16, name="ident_bf16")
-        bias_rows = keep.tile([P, BANK], BF16, name="bias_rows")
-        bias_all = keep.tile([P, GROUPS, OUT], BF16, name="bias_all")
-        x_codes = keep.tile([P, GROUPS * PASSES * P], U32, name="x_codes", align_bytes=64)
-        x_planes = keep.tile([P, GROUPS * PASSES * P], U8, name="x_planes", align_bytes=64)
+        x_all = keep.tile([P, GROUPS * IN], BF16, name="x_all", align_bytes=ALIGN)
+        ident_f32 = keep.tile([P, P], F32, name="ident_f32", align_bytes=ALIGN)
+        ident_bf16 = keep.tile([P, P], BF16, name="ident_bf16", align_bytes=ALIGN)
+        bias_rows = keep.tile([P, BANK], BF16, name="bias_rows", align_bytes=ALIGN)
+        bias_all = keep.tile([P, GROUPS, OUT], BF16, name="bias_all", align_bytes=ALIGN)
+        x_codes = keep.tile([P, GROUPS * PASSES * P], U32, name="x_codes", align_bytes=ALIGN)
+        x_planes = keep.tile([P, GROUPS * PASSES * P], U8, name="x_planes", align_bytes=ALIGN)
         w_planes = [
-            keep.tile([P, PASSES, OUT], U8, name="w_planes%d" % e, align_bytes=64) for e in range(GROUPS)
+            keep.tile([P, PASSES, OUT], U8, name="w_planes%d" % e, align_bytes=ALIGN) for e in range(GROUPS)
         ]
-        y_all = keep.tile([P, GROUPS, OUT], F32, name="y_all")
+        y_all = keep.tile([P, GROUPS, OUT], F32, name="y_all", align_bytes=ALIGN)
 
         make_identity(nc, ident_f32[:])
         make_identity(nc, ident_bf16[:])
@@ -82,9 +83,9 @@ def tile_groupedlinear_w_e_kernel(tc, x, W_words, W_scales, b, out):
                 tiles.append([])
                 for g in range(e * PASSES, (e + 1) * PASSES):
                     if len(chunks) == CHUNKS:
-                        words = word_pool.tile([P, width], U8, name="words", tag="words", align_bytes=64)
+                        words = word_pool.tile([P, width], U8, name="words", tag="words", align_bytes=ALIGN)
                     else:
-                        words = part_pool.tile([P, width], U8, name="words", tag="words%d" % part, align_bytes=64)
+                        words = part_pool.tile([P, width], U8, name="words", tag="words%d" % part, align_bytes=ALIGN)
                     nc.sync.dma_start(
                         out=words[:].bitcast(I32),
                         in_=W_words[g, :, first_byte : first_byte + width].bitcast(I32),
@@ -123,7 +124,7 @@ def tile_groupedlinear_w_e_kernel(tc, x, W_words, W_scales, b, out):
                         x_words[:, 256 * g + u : 256 * (g + 1) : 2],
                         ident_f32[:],
                     )
-            grouped = grouped_pool.tile([P, 2 * K_PASS], BF16, name="grouped", tag="grouped", align_bytes=64)
+            grouped = grouped_pool.tile([P, 2 * K_PASS], BF16, name="grouped", tag="grouped", align_bytes=ALIGN)
             dst = grouped[:].bitcast(F32).rearrange("p (s r u) -> p s r u", s=2, u=2)
             src = xt[:].rearrange("p (s u r) -> p s r u", s=2, u=2)
             if j % 2 == 0:
@@ -171,7 +172,7 @@ def tile_groupedlinear_w_e_kernel(tc, x, W_words, W_scales, b, out):
                         out=y_all[:, e, cols], in0=acc[i][:], in1=bias_all[:, e, cols], op=mybir.AluOpType.add
                     )
                     if e == GROUPS - 1:
-                        shuffled = out_pool.tile([P, GROUPS * BANK], F32, name="shuffled", tag="shuffled")
+                        shuffled = out_pool.tile([P, GROUPS * BANK], F32, name="shuffled", tag="shuffled", align_bytes=ALIGN)
                         dst = shuffled[:].rearrange("p (h e) -> p h e", e=GROUPS)
                         src = y_all[:, :, cols].rearrange("p e h -> p h e")
                         if c % 2 == 0:

@@ -22,6 +22,8 @@ CHUNKS = OUT // BANK
 PAIRS = GROUPS * PASSES // 2
 WORD_BUFS = 7
 LAST_SPLIT = (4, 2)
+BIAS_ROWS = 16
+BIAS_WIDTH = GROUPS * OUT // BIAS_ROWS
 ALIGN = 256
 LAST_RUN_PASSES = 3
 
@@ -46,7 +48,7 @@ def tile_groupedlinear_w_e_kernel(tc, x, W_words, W_scales, b, out):
         x_all = keep.tile([P, GROUPS * IN], BF16, name="x_all", align_bytes=ALIGN)
         ident_f32 = keep.tile([P, P], F32, name="ident_f32", align_bytes=ALIGN)
         ident_bf16 = keep.tile([P, P], BF16, name="ident_bf16", align_bytes=ALIGN)
-        bias_rows = keep.tile([P, BANK], BF16, name="bias_rows", align_bytes=ALIGN)
+        bias_rows = keep.tile([P, BIAS_WIDTH], BF16, name="bias_rows", align_bytes=ALIGN)
         bias_all = keep.tile([P, GROUPS, OUT], BF16, name="bias_all", align_bytes=ALIGN)
         x_codes = keep.tile([P, GROUPS * PASSES * P], U32, name="x_codes", align_bytes=ALIGN)
         x_planes = keep.tile([P, GROUPS * PASSES * P], U8, name="x_planes", align_bytes=ALIGN)
@@ -100,9 +102,7 @@ def tile_groupedlinear_w_e_kernel(tc, x, W_words, W_scales, b, out):
         for e in range(GROUPS - 1):
             load_scale_rows(e, 0, PASSES)
         load_scale_rows(GROUPS - 1, 0, PASSES - LAST_RUN_PASSES)
-        nc.sync.dma_start(
-            out=bias_rows[0 : GROUPS * CHUNKS, :], in_=b.rearrange("e (c n) -> (e c) n", n=BANK)
-        )
+        nc.sync.dma_start(out=bias_rows[0:BIAS_ROWS, :], in_=b.rearrange("e (c n) -> (e c) n", n=BIAS_WIDTH))
         load_scale_rows(GROUPS - 1, PASSES - LAST_RUN_PASSES, PASSES)
         word_tiles = [load_group_words(e) for e in range(GROUPS)]
 
@@ -136,20 +136,21 @@ def tile_groupedlinear_w_e_kernel(tc, x, W_words, W_scales, b, out):
             waiting = grouped
         quantise_pair(PAIRS - 1, waiting)
 
-        for k in range(GROUPS * CHUNKS):
+        bias_flat = bias_all[:].rearrange("p e h -> p (e h)")
+        for k in range(BIAS_ROWS):
             spread = psum.tile([P, BANK], F32, name="spread", tag="bank")
             nc.tensor.matmul(
-                out=spread[:],
+                out=spread[:, 0:BIAS_WIDTH],
                 lhsT=ident_bf16[:, k : k + 1].to_broadcast([P, P]),
                 rhs=bias_rows[:],
                 start=True,
                 stop=True,
             )
-            dst = bias_all[:, k // CHUNKS, (k % CHUNKS) * BANK : (k % CHUNKS + 1) * BANK]
+            dst = bias_flat[:, k * BIAS_WIDTH : (k + 1) * BIAS_WIDTH]
             if k % 2 == 0:
-                nc.scalar.copy(out=dst, in_=spread[:])
+                nc.scalar.copy(out=dst, in_=spread[:, 0:BIAS_WIDTH])
             else:
-                nc.vector.tensor_copy(out=dst, in_=spread[:])
+                nc.vector.tensor_copy(out=dst, in_=spread[:, 0:BIAS_WIDTH])
 
         for e in range(GROUPS):
             for part, chunks in enumerate(column_parts(e)):

from contextlib import ExitStack

import concourse.mybir as mybir
from concourse.masks import make_identity

F32 = mybir.dt.float32
BF16 = mybir.dt.bfloat16
I32 = mybir.dt.int32
U8 = mybir.dt.uint8
U32 = mybir.dt.uint32
FP8X4 = mybir.dt.float8_e4m3fn_x4
FP4X4 = mybir.dt.float4_e2m1fn_x4

P = 128
GROUPS = 2
IN = 4096
OUT = 3072
K_PASS = 512
PASSES = IN // K_PASS
BANK = 512
CHUNKS = OUT // BANK
PAIRS = GROUPS * PASSES // 2
WORD_BUFS = 7
LAST_SPLIT = (4, 2)
BIAS_ROWS = 16
BIAS_WIDTH = GROUPS * OUT // BIAS_ROWS
ALIGN = 256
LAST_RUN_PASSES = 3

FLOPS = 2 * P * GROUPS * IN * OUT


def tile_groupedlinear_w_e_kernel(tc, x, W_words, W_scales, b, out):
    nc = tc.nc
    x_rows = x.flatten_outer_dims()
    out_rows = out.flatten_outer_dims()
    scale_rows = W_scales.bitcast(I32).rearrange("g q n -> q g n")

    with ExitStack() as ctx:
        ctx.enter_context(tc.manual_schedule())
        keep = ctx.enter_context(tc.tile_pool(name="keep", bufs=1))
        grouped_pool = ctx.enter_context(tc.tile_pool(name="grouped_pool", bufs=3))
        word_pool = ctx.enter_context(tc.tile_pool(name="word_pool", bufs=WORD_BUFS))
        part_pool = ctx.enter_context(tc.tile_pool(name="part_pool", bufs=PASSES))
        out_pool = ctx.enter_context(tc.tile_pool(name="out_pool", bufs=CHUNKS))
        psum = ctx.enter_context(tc.psum_pool(name="psum", bufs=8))

        x_all = keep.tile([P, GROUPS * IN], BF16, name="x_all", align_bytes=ALIGN)
        ident_f32 = keep.tile([P, P], F32, name="ident_f32", align_bytes=ALIGN)
        ident_bf16 = keep.tile([P, P], BF16, name="ident_bf16", align_bytes=ALIGN)
        bias_rows = keep.tile([P, BIAS_WIDTH], BF16, name="bias_rows", align_bytes=ALIGN)
        bias_all = keep.tile([P, GROUPS, OUT], BF16, name="bias_all", align_bytes=ALIGN)
        x_codes = keep.tile([P, GROUPS * PASSES * P], U32, name="x_codes", align_bytes=ALIGN)
        x_planes = keep.tile([P, GROUPS * PASSES * P], U8, name="x_planes", align_bytes=ALIGN)
        w_planes = [
            keep.tile([P, PASSES, OUT], U8, name="w_planes%d" % e, align_bytes=ALIGN) for e in range(GROUPS)
        ]
        y_all = keep.tile([P, GROUPS, OUT], F32, name="y_all", align_bytes=ALIGN)

        make_identity(nc, ident_f32[:])
        make_identity(nc, ident_bf16[:])

        def zero_scale_planes(e):
            nc.vector.memset(w_planes[e][:].bitcast(I32), 0)

        def load_scale_rows(e, first, last):
            for half in range(2):
                for r in range(4):
                    nc.sync.dma_start(
                        out=w_planes[e][32 * half + r : P : 64, first:last, :].bitcast(I32),
                        in_=scale_rows[4 * half + r : 16 : 8, e * PASSES + first : e * PASSES + last, :],
                    )

        def column_parts(e):
            if e < GROUPS - 1:
                return [range(CHUNKS)]
            firsts = [sum(LAST_SPLIT[:i]) for i in range(len(LAST_SPLIT))]
            return [range(first, first + count) for first, count in zip(firsts, LAST_SPLIT)]

        def load_group_words(e):
            tiles = []
            for part, chunks in enumerate(column_parts(e)):
                first_byte = chunks.start * 2 * BANK
                width = len(chunks) * 2 * BANK
                tiles.append([])
                for g in range(e * PASSES, (e + 1) * PASSES):
                    if len(chunks) == CHUNKS:
                        words = word_pool.tile([P, width], U8, name="words", tag="words", align_bytes=ALIGN)
                    else:
                        words = part_pool.tile([P, width], U8, name="words", tag="words%d" % part, align_bytes=ALIGN)
                    nc.sync.dma_start(
                        out=words[:].bitcast(I32),
                        in_=W_words[g, :, first_byte : first_byte + width].bitcast(I32),
                    )
                    tiles[-1].append(words)
            return tiles

        nc.sync.dma_start(out=x_all[:], in_=x_rows)
        nc.vector.memset(bias_rows[:], 0.0)
        for e in range(GROUPS):
            zero_scale_planes(e)
        for e in range(GROUPS - 1):
            load_scale_rows(e, 0, PASSES)
        load_scale_rows(GROUPS - 1, 0, PASSES - LAST_RUN_PASSES)
        nc.sync.dma_start(out=bias_rows[0:BIAS_ROWS, :], in_=b.rearrange("e (c n) -> (e c) n", n=BIAS_WIDTH))
        load_scale_rows(GROUPS - 1, PASSES - LAST_RUN_PASSES, PASSES)
        word_tiles = [load_group_words(e) for e in range(GROUPS)]

        def quantise_pair(j, grouped):
            cols = slice(j * 2 * P, (j + 1) * 2 * P)
            nc.vector.quantize_mx(
                out=x_codes[:, cols].bitcast(FP8X4), scales=x_planes[:, cols], in_=grouped[:]
            )

        x_words = x_all[:].bitcast(F32)
        waiting = None
        for j in range(PAIRS):
            xt = psum.tile([P, BANK], F32, name="xt", tag="bank")
            for s in range(2):
                g = 2 * j + s
                for u in range(2):
                    nc.tensor.transpose(
                        xt[:, (2 * s + u) * P : (2 * s + u + 1) * P],
                        x_words[:, 256 * g + u : 256 * (g + 1) : 2],
                        ident_f32[:],
                    )
            grouped = grouped_pool.tile([P, 2 * K_PASS], BF16, name="grouped", tag="grouped", align_bytes=ALIGN)
            dst = grouped[:].bitcast(F32).rearrange("p (s r u) -> p s r u", s=2, u=2)
            src = xt[:].rearrange("p (s u r) -> p s r u", s=2, u=2)
            if j % 2 == 0:
                nc.scalar.copy(out=dst, in_=src)
            else:
                nc.vector.tensor_copy(out=dst, in_=src)
            if waiting is not None:
                quantise_pair(j - 1, waiting)
            waiting = grouped
        quantise_pair(PAIRS - 1, waiting)

        bias_flat = bias_all[:].rearrange("p e h -> p (e h)")
        for k in range(BIAS_ROWS):
            spread = psum.tile([P, BANK], F32, name="spread", tag="bank")
            nc.tensor.matmul(
                out=spread[:, 0:BIAS_WIDTH],
                lhsT=ident_bf16[:, k : k + 1].to_broadcast([P, P]),
                rhs=bias_rows[:],
                start=True,
                stop=True,
            )
            dst = bias_flat[:, k * BIAS_WIDTH : (k + 1) * BIAS_WIDTH]
            if k % 2 == 0:
                nc.scalar.copy(out=dst, in_=spread[:, 0:BIAS_WIDTH])
            else:
                nc.vector.tensor_copy(out=dst, in_=spread[:, 0:BIAS_WIDTH])

        for e in range(GROUPS):
            for part, chunks in enumerate(column_parts(e)):
                acc = [psum.tile([P, BANK], F32, name="acc", tag="bank") for c in chunks]
                for s in range(PASSES):
                    g = e * PASSES + s
                    for i, c in enumerate(chunks):
                        nc.tensor.matmul_mx(
                            out=acc[i][:],
                            lhsT=x_codes[:, g * P : (g + 1) * P].bitcast(FP8X4),
                            lhsT_scale=x_planes[:, g * P : (g + 1) * P],
                            rhs=word_tiles[e][part][s][:, i * 2 * BANK : (i + 1) * 2 * BANK].bitcast(FP4X4),
                            rhs_scale=w_planes[e][:, s, c * BANK : (c + 1) * BANK],
                            start=(s == 0),
                            stop=(s == PASSES - 1),
                        )
                for i, c in enumerate(chunks):
                    cols = slice(c * BANK, (c + 1) * BANK)
                    nc.vector.tensor_tensor(
                        out=y_all[:, e, cols], in0=acc[i][:], in1=bias_all[:, e, cols], op=mybir.AluOpType.add
                    )
                    if e == GROUPS - 1:
                        shuffled = out_pool.tile([P, GROUPS * BANK], F32, name="shuffled", tag="shuffled", align_bytes=ALIGN)
                        dst = shuffled[:].rearrange("p (h e) -> p h e", e=GROUPS)
                        src = y_all[:, :, cols].rearrange("p e h -> p h e")
                        if c % 2 == 0:
                            nc.scalar.copy(out=dst, in_=src)
                        else:
                            nc.vector.tensor_copy(out=dst, in_=src)
                        nc.sync.dma_start(
                            out=out_rows[:, c * GROUPS * BANK : (c + 1) * GROUPS * BANK], in_=shuffled[:]
                        )
